import numpy as np
import ml_dtypes


def mxq(x, axis, fmt="e4m3"):
    dtype, down = {"e4m3": (ml_dtypes.float8_e4m3fn, 7), "e5m2": (ml_dtypes.float8_e5m2, 14)}[fmt]
    v = np.moveaxis(np.asarray(x, np.float32).astype(ml_dtypes.bfloat16).astype(np.float64), axis, -1)
    blocks = v.reshape(v.shape[:-1] + (-1, 32))
    amax = np.abs(blocks).max(-1, keepdims=True)
    byte = np.maximum(np.where(amax > 0, np.frexp(amax)[1] - 1 + 127, 0) - down, 1)
    scale = np.exp2(byte - 127.0)
    codes = (blocks / scale).astype(np.float32).astype(dtype).astype(np.float64)
    return np.moveaxis((codes * scale).reshape(v.shape), -1, axis)


WIDE = False


def mx_kscale(k):
    if not WIDE:
        return np.ones(k)
    levels = np.array([10, -10, 5, -5, 0])
    if k % 512:
        return np.exp2(np.random.permutation(np.resize(levels, k // 32))).repeat(32)
    a = np.empty((k // 512, 16))
    for p in range(k // 512):
        a[p, :8] = np.random.permutation(np.resize(levels, 8))
        for g in range(8):
            far = levels[np.abs(levels - a[p, g]) >= 10]
            a[p, g + 8] = far[np.random.randint(len(far))]
    return np.exp2(a.ravel()).repeat(32)


BF16 = ml_dtypes.bfloat16


def bf(x):
    return np.asarray(x, np.float32).astype(BF16)


def f64(x):
    return np.asarray(x).astype(np.float64)


N, B, A, C, D, NR, XD = 4, 1024, 512, 64, 1024, 8, 3
GAMMA = 6.125


def setup_inputs():
    s = mx_kscale(A)
    t = mx_kscale(C * NR)[::NR]
    return {"input": bf(np.exp(np.random.standard_normal((N, C, A))) * 16.0 / A * s * t[:, None]),
            "difference_mat": bf(np.random.standard_normal((N, B, A, XD))),
            "relative_mask": bf(np.random.random((N, B, A)) / s),
            "W": bf(np.random.standard_normal((D, C, NR)) / np.sqrt(C * NR) / t[:, None]),
            "radii": bf(np.random.random(NR) * 2.0)}


def reference(input, difference_mat, relative_mask, W, radii):
    dm = f64(difference_mat)
    dist = np.sqrt(np.sum(dm * dm, axis=-1))
    R = np.exp(-GAMMA * (dist[..., None] - f64(radii)) ** 2)
    R = R * f64(relative_mask)[..., None]
    Rk = R.transpose(0, 2, 1, 3).reshape(N, A, B * NR)
    T = mxq(f64(input), 2, "e4m3") @ mxq(Rk, 1, "e4m3")
    Tk = T.reshape(N, C, B, NR).transpose(0, 1, 3, 2).reshape(N, C * NR, B)
    return mxq(f64(W).reshape(D, C * NR), 1, "e4m3") @ mxq(Tk, 1, "e4m3")

@@ -1,0 +1,352 @@
+from contextlib import ExitStack
+
+import concourse.bass as bass
+import concourse.mybir as mybir
+import concourse.tile as tile
+from concourse.masks import make_identity
+
+F32 = mybir.dt.float32
+BF16 = mybir.dt.bfloat16
+U32 = mybir.dt.uint32
+U8 = mybir.dt.uint8
+I32 = mybir.dt.int32
+FP8X4 = mybir.dt.float8_e4m3fn_x4
+ACT = mybir.ActivationFunctionType
+ALU = mybir.AluOpType
+
+NCLOUD, B, A, C, D, NR, XD = 4, 1024, 512, 64, 1024, 8, 3
+GAMMA = 6.125
+P = 128
+NT = A // P
+G, J = 16, 8
+CH = 128
+CPN = B // CH
+NCH = NCLOUD * CPN
+COLS = CH * NT
+S_RADII = 5
+FLOPS = 2 * NCLOUD * C * A * B * NR + 2 * NCLOUD * D * C * NR * B
+
+
+def tile_se3pointconvolution_t_kernel(tc, feat, diff, mask, w, radii, out):
+    nc = tc.nc
+    with ExitStack() as ctx:
+        ctx.enter_context(tc.manual_schedule())
+        const = ctx.enter_context(tc.tile_pool(name="const", bufs=1))
+        dpool = ctx.enter_context(tc.tile_pool(name="dist", bufs=1))
+        keep = ctx.enter_context(tc.tile_pool(name="keep", bufs=1))
+        stage = ctx.enter_context(tc.tile_pool(name="stage", bufs=2))
+        mraw_pool = ctx.enter_context(tc.tile_pool(name="mraw", bufs=2))
+
+        one = const.tile([P, 1], F32, name="one")
+        junk = const.tile([P, 1], F32, name="junk")
+        rad_b = const.tile([P, NR], BF16, name="rad_b")
+        negr = const.tile([P, NR], F32, name="negr")
+        ident_f = const.tile([P, P], F32, name="ident_f")
+        ident_b = const.tile([P, P], BF16, name="ident_b")
+        nc.scalar.dma_start(out=rad_b[:], in_=radii.partition_broadcast(P))
+        zeros = const.tile([P, 512], BF16, name="zeros")
+        nc.vector.memset(one[:], 1.0)
+        nc.vector.memset(zeros[:], 0.0)
+        nc.scalar.activation(out=junk[:], in_=one[:], func=ACT.Sqrt)
+        make_identity(nc, ident_f[:])
+        make_identity(nc, ident_b[:])
+
+        wtmp = stage.tile([P, 8192], BF16, tag="stage", name="wtmp", align_bytes=64)
+        itmp = stage.tile([P, 8192], BF16, tag="stage", name="itmp", align_bytes=64)
+        nc.vector.memset(itmp[:, 4096:8192].bitcast(I32), 0)
+        nc.vector.tensor_scalar(out=negr[:], in0=rad_b[:], scalar1=-1.0, scalar2=None, op0=ALU.mult)
+
+        w_codes = keep.tile([P, D], U32, name="w_codes", align_bytes=64)
+        w_scales = keep.tile([P, D], U8, name="w_scales", align_bytes=64)
+        in_codes = keep.tile([P, 1024], U32, name="in_codes", align_bytes=64)
+        in_scales = keep.tile([P, 1024], U8, name="in_scales", align_bytes=64)
+
+        dist = [dpool.tile([P, COLS], F32, name="dist%d" % i) for i in range(NCH)]
+        mraw = {}
+        mperm = {}
+
+        def load_mask(h):
+            t = mraw_pool.tile([P, 4, A], BF16, tag="mraw", name="mraw%d" % h)
+            nc.sync.dma_start(
+                out=t[:],
+                in_=mask[h // 2, (h % 2) * 512 : (h % 2 + 1) * 512, :].rearrange("(j p) a -> p j a", p=P),
+            )
+            mraw[h] = t
+
+        def permute_mask(h):
+            t = mraw_pool.tile([P, NT, 4 * P], BF16, tag="mperm", name="mperm%d" % h)
+            nc.vector.tensor_copy(
+                out=t[:].rearrange("p t (n j) -> p t n j", j=J),
+                in_=mraw[h][:].rearrange("p b (g t j) -> p t (b g) j", t=NT, j=J),
+            )
+            mperm[h] = t
+
+        with tc.tile_pool(name="dm", bufs=6) as dmp, tc.tile_pool(name="sq", bufs=4) as sqp, tc.psum_pool(
+            name="pps", bufs=4
+        ) as pps:
+            dm = {}
+            sq = {}
+            st = {}
+
+            def load_dm(i):
+                t = dmp.tile([P, A * XD], BF16, tag="dm", name="dm%d" % i)
+                nc.sync.dma_start(
+                    out=t[:], in_=diff[i // CPN, (i % CPN) * CH : (i % CPN + 1) * CH].rearrange("b a x -> b (a x)")
+                )
+                dm[i] = t
+
+            def squares(i):
+                v = dm[i][:].rearrange("p (g t j x) -> p x t g j", g=G, t=NT, j=J)
+                s = sqp.tile([P, XD, A], F32, tag="sq", name="sq%d" % i)
+                so = [s[:, x, :].rearrange("p (t g j) -> p t g j", t=NT, g=G) for x in range(XD)]
+                for x in range(2):
+                    nc.vector.tensor_tensor(out=so[x], in0=v[:, x], in1=v[:, x], op=ALU.mult)
+                nc.scalar.activation(out=so[2], in_=v[:, 2], func=ACT.Square)
+                sq[i] = s
+
+            def keep_clock(n):
+                nc.tensor.matmul(out=warm[:, 0:n], lhsT=ident_b[:], rhs=zeros[:, 0:n], start=True, stop=True)
+
+            def sum_transpose(i):
+                t_ps = pps.tile([P, NT, CH], F32, tag="st", name="st%d" % i)
+                for t in range(NT):
+                    for x in range(XD):
+                        nc.tensor.matmul(
+                            out=t_ps[:, t, :],
+                            lhsT=sq[i][:, x, t * P : (t + 1) * P],
+                            rhs=ident_f[:],
+                            is_transpose=True,
+                            start=(x == 0),
+                            stop=(x == XD - 1),
+                        )
+                keep_clock(256)
+                st[i] = t_ps
+
+            def root(i):
+                nc.scalar.activation(
+                    out=dist[i][:].rearrange("p (b t) -> p b t", t=NT),
+                    in_=st[i][:].rearrange("p t b -> p b t"),
+                    func=ACT.Sqrt,
+                )
+
+            warm = pps.tile([P, 512], F32, tag="warm", name="warm", bufs=1)
+            for i in range(5):
+                load_dm(i)
+            for i in range(8):
+                keep_clock(512)
+            for i in range(NCH + 2):
+                if i + 5 < NCH:
+                    load_dm(i + 5)
+                if i < NCH:
+                    squares(i)
+                if 1 <= i <= NCH:
+                    sum_transpose(i - 1)
+                if i >= 2:
+                    root(i - 2)
+
+            nc.sync.dma_start(
+                out=itmp[:, 0:1024].rearrange("p (j a) -> p j a", j=2),
+                in_=feat.rearrange("n c a -> (n c) a").rearrange("(j p) a -> p j a", p=P),
+            )
+            nc.sync.dma_start(
+                out=wtmp[:, 0:4096].rearrange("p (e k) -> p e k", e=8),
+                in_=w.rearrange("(e p) c r -> p e (c r)", p=P),
+            )
+            for h in range(2):
+                load_mask(h)
+            nc.vector.tensor_copy(
+                out=itmp[:, 1024:2048].rearrange("p (t n j) -> p t n j", t=NT, j=J),
+                in_=itmp[:, 0:1024].rearrange("p (n t j) -> p t n j", t=NT, j=J),
+            )
+
+            inq = itmp[:, 4096:8192].rearrange("p (n h c two t) -> p n h c two t", n=NCLOUD, h=2, c=C, two=2)
+            for j in range(2):
+                ips = pps.tile([P, NT, P], BF16, tag="prep", name="ips%d" % j, bufs=3)
+                for t in range(NT):
+                    nc.tensor.transpose(
+                        out=ips[:, t, :], in_=itmp[:, 1024 + t * 256 + j * P : 1024 + t * 256 + (j + 1) * P], identity=ident_b[:]
+                    )
+                for n2 in range(2):
+                    for h in range(2):
+                        nc.vector.tensor_copy(
+                            out=inq[:, 2 * j + n2, h, :, h, :],
+                            in_=ips[:, :, n2 * C : (n2 + 1) * C].rearrange("p t c -> p c t"),
+                        )
+            w_words = wtmp[:, 0:4096].bitcast(F32).rearrange("p (e q u) -> p e u q", e=8, u=2)
+            w_grouped = wtmp[:, 4096:8192].bitcast(F32).rearrange("p (e d u) -> p e d u", e=8, u=2)
+            for k in range(4):
+                wps = pps.tile([P, 2, 2, P], F32, tag="prep", name="wps%d" % k, bufs=3)
+                for e in range(2):
+                    for u in range(2):
+                        nc.tensor.transpose(out=wps[:, e, u, :], in_=w_words[:, 2 * k + e, u, :], identity=ident_f[:])
+                nc.vector.tensor_copy(
+                    out=w_grouped[:, 2 * k : 2 * k + 2, :, :], in_=wps[:].rearrange("p e u d -> p e d u")
+                )
+                if k == 0:
+                    nc.vector.quantize_mx(
+                        out=in_codes[:].bitcast(FP8X4), scales=in_scales[:], in_=itmp[:, 4096:8192]
+                    )
+            nc.vector.quantize_mx(out=w_codes[:].bitcast(FP8X4), scales=w_scales[:], in_=wtmp[:, 4096:8192])
+            for h in range(2):
+                permute_mask(h)
+                load_mask(h + 2)
+
+        zp = ctx.enter_context(tc.tile_pool(name="z", bufs=4))
+        yp = ctx.enter_context(tc.tile_pool(name="y", bufs=2))
+        rp = ctx.enter_context(tc.tile_pool(name="r", bufs=2))
+        tp = ctx.enter_context(tc.tile_pool(name="t", bufs=2))
+        ps_m = ctx.enter_context(tc.psum_pool(name="ps_m", bufs=2))
+        ps_t = ctx.enter_context(tc.psum_pool(name="ps_t", bufs=2))
+        ps_o = ctx.enter_context(tc.psum_pool(name="ps_o", bufs=2))
+
+        z = {}
+        mt = {}
+        rb = {}
+        rc = {}
+        tps = {}
+        tb = {}
+        tcd = {}
+        ops = {}
+        sto = {}
+        G_RADII = NR - S_RADII
+
+        def pool_squares(i):
+            zt = zp.tile([P, NR, COLS], F32, tag="z", name="z%d" % i)
+            y = yp.tile([P, G_RADII, COLS], F32, tag="y", name="y%d" % i)
+            for g in range(G_RADII):
+                r = S_RADII + g
+                nc.gpsimd.tensor_scalar(
+                    out=y[:, g, :], in0=dist[i][:], scalar1=negr[:, r : r + 1], scalar2=1.0, op0=ALU.add, op1=ALU.mult
+                )
+            nc.gpsimd.tensor_tensor(out=zt[:, S_RADII:NR, :], in0=y[:], in1=y[:], op=ALU.mult)
+            z[i] = zt
+
+        def act_squares(i):
+            for r in range(S_RADII):
+                nc.scalar.activation(
+                    out=z[i][:, r, :], in_=dist[i][:], func=ACT.Square, bias=negr[:, r : r + 1], scale=1.0
+                )
+
+        def act_exp(i, h):
+            nc.scalar.activation(
+                out=z[i][:, 4 * h : 4 * h + 4, :], in_=z[i][:, 4 * h : 4 * h + 4, :], func=ACT.Exp, scale=-GAMMA
+            )
+
+        def mask_transpose(i):
+            m = ps_m.tile([P, NT, CH], BF16, tag="mt", name="mt%d" % i)
+            for t in range(NT):
+                nc.tensor.transpose(
+                    out=m[:, t, :], in_=mperm[i // 4][:, t, (i % 4) * P : (i % 4 + 1) * P], identity=ident_b[:]
+                )
+            mt[i] = m
+
+        def weigh(i, h):
+            if h == 0:
+                rb[i] = rp.tile([P, NR * COLS], BF16, tag="rb", name="rb%d" % i, align_bytes=64)
+            nc.vector.tensor_tensor(
+                out=rb[i][:, h * 2048 : (h + 1) * 2048].rearrange("p (b r t) -> p b r t", r=4, t=NT),
+                in0=z[i][:, 4 * h : 4 * h + 4, :].rearrange("p r (b t) -> p b r t", t=NT),
+                in1=mt[i][:].rearrange("p t b -> p b t").unsqueeze(2).to_broadcast([P, CH, 4, NT]),
+                op=ALU.mult,
+            )
+
+        def quant_r(i):
+            codes = rp.tile([P, 1024], U32, tag="rc", name="rc%d" % i, align_bytes=64)
+            scales = rp.tile([P, 1024], U8, tag="rs", name="rs%d" % i, align_bytes=64)
+            nc.vector.quantize_mx(out=codes[:].bitcast(FP8X4), scales=scales[:], in_=rb[i][:])
+            rc[i] = (codes, scales)
+
+        def matmul_one(i):
+            n = i // CPN
+            acc = ps_t.tile([P, 512], F32, tag="tps", name="tps%d" % i)
+            codes, scales = rc[i]
+            for h in range(2):
+                lo = (2 * n + h) * P
+                nc.tensor.matmul_mx(
+                    out=acc[:],
+                    lhsT=in_codes[:, lo : lo + P].bitcast(FP8X4),
+                    lhsT_scale=in_scales[:, lo : lo + P],
+                    rhs=codes[:, h * 512 : (h + 1) * 512].bitcast(FP8X4),
+                    rhs_scale=scales[:, h * 512 : (h + 1) * 512],
+                    start=(h == 0),
+                    stop=(h == 1),
+                )
+            tps[i] = acc
+
+        def t_out(i):
+            t = tp.tile([P, 512], BF16, tag="tb", name="tb%d" % i, align_bytes=64)
+            nc.vector.tensor_copy(out=t[:], in_=tps[i][:])
+            tb[i] = t
+
+        def quant_t(i):
+            codes = tp.tile([P, CH], U32, tag="tc", name="tc%d" % i, align_bytes=64)
+            scales = tp.tile([P, CH], U8, tag="ts", name="ts%d" % i, align_bytes=64)
+            nc.vector.quantize_mx(out=codes[:].bitcast(FP8X4), scales=scales[:], in_=tb[i][:])
+            tcd[i] = (codes, scales)
+
+        def matmul_two(i):
+            codes, scales = tcd[i]
+            banks = []
+            for k in range(2):
+                o = ps_o.tile([P, 4, CH], F32, tag="o%d" % k, name="o%d_%d" % (k, i))
+                for e in range(4):
+                    lo = (4 * k + e) * P
+                    nc.tensor.matmul_mx(
+                        out=o[:, e, :],
+                        lhsT=w_codes[:, lo : lo + P].bitcast(FP8X4),
+                        lhsT_scale=w_scales[:, lo : lo + P],
+                        rhs=codes[:].bitcast(FP8X4),
+                        rhs_scale=scales[:],
+                        start=True,
+                        stop=True,
+                    )
+                banks.append(o)
+            ops[i] = banks
+
+        def o_out(i, engines):
+            hf = i // 4
+            if i % 4 == 0:
+                sto[hf] = stage.tile([P, 8, 512], F32, tag="stage", name="sto%d" % hf, align_bytes=64)
+            cols = slice((i % 4) * CH, (i % 4 + 1) * CH)
+            for k in range(2):
+                if engines[k] == "v":
+                    nc.vector.tensor_copy(out=sto[hf][:, 4 * k : 4 * k + 4, cols], in_=ops[i][k][:])
+                else:
+                    nc.scalar.copy(out=sto[hf][:, 4 * k : 4 * k + 4, cols], in_=ops[i][k][:])
+            dst = out[hf // 2].rearrange("(e p) b -> p e b", p=P)
+            base = (hf % 2) * 512
+            if hf == 7:
+                nc.sync.dma_start(out=dst[:, :, base + (i % 4) * CH : base + (i % 4 + 1) * CH], in_=sto[hf][:, :, cols])
+            elif i % 4 == 3:
+                nc.sync.dma_start(out=dst[:, :, base : base + 512], in_=sto[hf][:])
+
+        pool_squares(0)
+        mask_transpose(0)
+        for i in range(NCH + 2):
+            if i + 1 < NCH:
+                pool_squares(i + 1)
+            if i < NCH:
+                act_squares(i)
+                act_exp(i, 0)
+                act_exp(i, 1)
+            if 1 <= i <= NCH:
+                matmul_one(i - 1)
+            if i + 1 < NCH:
+                mask_transpose(i + 1)
+            if i < NCH:
+                weigh(i, 0)
+            if 1 <= i <= NCH:
+                t_out(i - 1)
+            if i < NCH:
+                weigh(i, 1)
+            if 1 <= i <= NCH:
+                quant_t(i - 1)
+                matmul_two(i - 1)
+            if i < NCH:
+                quant_r(i)
+            if i % 4 == 1 and 2 <= (i + 3) // 4 < 8:
+                permute_mask((i + 3) // 4)
+                if (i + 3) // 4 + 2 < 8:
+                    load_mask((i + 3) // 4 + 2)
+            if i >= 2:
+                o_out(i - 2, "vv" if i < NCH - 1 else ("ss" if i <= NCH else "vs"))

@@ -119,7 +119,7 @@ def tile_se3pointconvolution_t_kernel(tc, feat, diff, mask, w, radii, out):
                             start=(x == 0),
                             stop=(x == XD - 1),
                         )
-                keep_clock(256)
+                keep_clock(512)
                 st[i] = t_ps
 
             def root(i):
@@ -132,7 +132,7 @@ def tile_se3pointconvolution_t_kernel(tc, feat, diff, mask, w, radii, out):
             warm = pps.tile([P, 512], F32, tag="warm", name="warm", bufs=1)
             for i in range(5):
                 load_dm(i)
-            for i in range(8):
+            for i in range(4):
                 keep_clock(512)
             for i in range(NCH + 2):
                 if i + 5 < NCH:

@@ -322,31 +322,32 @@ def tile_se3pointconvolution_t_kernel(tc, feat, diff, mask, w, radii, out):
 
         pool_squares(0)
         mask_transpose(0)
-        for i in range(NCH + 2):
+        for i in range(NCH + 3):
             if i + 1 < NCH:
                 pool_squares(i + 1)
             if i < NCH:
                 act_squares(i)
                 act_exp(i, 0)
                 act_exp(i, 1)
-            if 1 <= i <= NCH:
-                matmul_one(i - 1)
             if i + 1 < NCH:
                 mask_transpose(i + 1)
             if i < NCH:
                 weigh(i, 0)
-            if 1 <= i <= NCH:
-                t_out(i - 1)
+            if 2 <= i <= NCH + 1:
+                t_out(i - 2)
             if i < NCH:
                 weigh(i, 1)
             if 1 <= i <= NCH:
-                quant_t(i - 1)
-                matmul_two(i - 1)
-            if i < NCH:
-                quant_r(i)
+                quant_r(i - 1)
+            if 2 <= i <= NCH + 1:
+                quant_t(i - 2)
             if i % 4 == 1 and 2 <= (i + 3) // 4 < 8:
                 permute_mask((i + 3) // 4)
                 if (i + 3) // 4 + 2 < 8:
                     load_mask((i + 3) // 4 + 2)
-            if i >= 2:
-                o_out(i - 2, "vv" if i < NCH - 1 else ("ss" if i <= NCH else "vs"))
+            if 1 <= i <= NCH:
+                matmul_one(i - 1)
+            if 2 <= i <= NCH + 1:
+                matmul_two(i - 2)
+            if i >= 3:
+                o_out(i - 3, "vs" if i % 2 or i >= NCH else "vv")

@@ -244,9 +244,9 @@ def tile_se3pointconvolution_t_kernel(tc, feat, diff, mask, w, radii, out):
             if h == 0:
                 rb[i] = rp.tile([P, NR * COLS], BF16, tag="rb", name="rb%d" % i, align_bytes=64)
             nc.vector.tensor_tensor(
-                out=rb[i][:, h * 2048 : (h + 1) * 2048].rearrange("p (b r t) -> p b r t", r=4, t=NT),
-                in0=z[i][:, 4 * h : 4 * h + 4, :].rearrange("p r (b t) -> p b r t", t=NT),
-                in1=mt[i][:].rearrange("p t b -> p b t").unsqueeze(2).to_broadcast([P, CH, 4, NT]),
+                out=rb[i][:, h * 2048 : (h + 1) * 2048].rearrange("p (r b t) -> p r b t", r=4, t=NT),
+                in0=z[i][:, 4 * h : 4 * h + 4, :].rearrange("p r (b t) -> p r b t", t=NT),
+                in1=mt[i][:].rearrange("p t b -> p b t").unsqueeze(1).to_broadcast([P, 4, CH, NT]),
                 op=ALU.mult,
             )
 
@@ -275,7 +275,9 @@ def tile_se3pointconvolution_t_kernel(tc, feat, diff, mask, w, radii, out):
 
         def t_out(i):
             t = tp.tile([P, 512], BF16, tag="tb", name="tb%d" % i, align_bytes=64)
-            nc.vector.tensor_copy(out=t[:], in_=tps[i][:])
+            nc.vector.tensor_copy(
+                out=t[:].rearrange("p (b r) -> p b r", r=4), in_=tps[i][:].rearrange("p (r b) -> p b r", r=4)
+            )
             tb[i] = t
 
         def quant_t(i):

@@ -23,7 +23,6 @@ CH = 128
 CPN = B // CH
 NCH = NCLOUD * CPN
 COLS = CH * NT
-S_RADII = 5
 FLOPS = 2 * NCLOUD * C * A * B * NR + 2 * NCLOUD * D * C * NR * B
 
 
@@ -208,21 +207,28 @@ def tile_se3pointconvolution_t_kernel(tc, feat, diff, mask, w, radii, out):
         tcd = {}
         ops = {}
         sto = {}
-        G_RADII = NR - S_RADII
+
+        def first_pool_radius(i):
+            return 5 + i % 2
 
         def pool_squares(i):
+            first = first_pool_radius(i)
             zt = zp.tile([P, NR, COLS], F32, tag="z", name="z%d" % i)
-            y = yp.tile([P, G_RADII, COLS], F32, tag="y", name="y%d" % i)
-            for g in range(G_RADII):
-                r = S_RADII + g
+            y = yp.tile([P, NR - first, COLS], F32, tag="y", name="y%d" % i)
+            for r in range(first, NR):
                 nc.gpsimd.tensor_scalar(
-                    out=y[:, g, :], in0=dist[i][:], scalar1=negr[:, r : r + 1], scalar2=1.0, op0=ALU.add, op1=ALU.mult
+                    out=y[:, r - first, :],
+                    in0=dist[i][:],
+                    scalar1=negr[:, r : r + 1],
+                    scalar2=1.0,
+                    op0=ALU.add,
+                    op1=ALU.mult,
                 )
-            nc.gpsimd.tensor_tensor(out=zt[:, S_RADII:NR, :], in0=y[:], in1=y[:], op=ALU.mult)
+            nc.gpsimd.tensor_tensor(out=zt[:, first:NR, :], in0=y[:], in1=y[:], op=ALU.mult)
             z[i] = zt
 
         def act_squares(i):
-            for r in range(S_RADII):
+            for r in range(first_pool_radius(i)):
                 nc.scalar.activation(
                     out=z[i][:, r, :], in_=dist[i][:], func=ACT.Square, bias=negr[:, r : r + 1], scale=1.0
                 )
@@ -352,4 +358,4 @@ def tile_se3pointconvolution_t_kernel(tc, feat, diff, mask, w, radii, out):
             if 2 <= i <= NCH + 1:
                 matmul_two(i - 2)
             if i >= 3:
-                o_out(i - 3, "vs" if i % 2 or i >= NCH else "vv")
+                o_out(i - 3, "vs" if i >= NCH else "vv")

@@ -198,6 +198,8 @@ def tile_se3pointconvolution_t_kernel(tc, feat, diff, mask, w, radii, out):
         ps_t = ctx.enter_context(tc.psum_pool(name="ps_t", bufs=2))
         ps_o = ctx.enter_context(tc.psum_pool(name="ps_o", bufs=2))
 
+        turns = ctx.enter_context(tc.tile_pool(name="turns", bufs=2))
+
         z = {}
         mt = {}
         rb = {}
@@ -209,9 +211,9 @@ def tile_se3pointconvolution_t_kernel(tc, feat, diff, mask, w, radii, out):
         sto = {}
 
         def first_pool_radius(i):
-            return 5 + i % 2
+            return 5
 
-        def pool_squares(i):
+        def pool_squares(i, turn):
             first = first_pool_radius(i)
             zt = zp.tile([P, NR, COLS], F32, tag="z", name="z%d" % i)
             y = yp.tile([P, NR - first, COLS], F32, tag="y", name="y%d" % i)
@@ -219,7 +221,7 @@ def tile_se3pointconvolution_t_kernel(tc, feat, diff, mask, w, radii, out):
                 nc.gpsimd.tensor_scalar(
                     out=y[:, r - first, :],
                     in0=dist[i][:],
-                    scalar1=negr[:, r : r + 1],
+                    scalar1=turn[:, r : r + 1],
                     scalar2=1.0,
                     op0=ALU.add,
                     op1=ALU.mult,
@@ -328,11 +330,10 @@ def tile_se3pointconvolution_t_kernel(tc, feat, diff, mask, w, radii, out):
             elif i % 4 == 3:
                 nc.sync.dma_start(out=dst[:, :, base : base + 512], in_=sto[hf][:])
 
-        pool_squares(0)
+        for i in range(3):
+            pool_squares(i, negr)
         mask_transpose(0)
         for i in range(NCH + 3):
-            if i + 1 < NCH:
-                pool_squares(i + 1)
             if i < NCH:
                 act_squares(i)
                 act_exp(i, 0)
@@ -353,9 +354,13 @@ def tile_se3pointconvolution_t_kernel(tc, feat, diff, mask, w, radii, out):
                 permute_mask((i + 3) // 4)
                 if (i + 3) // 4 + 2 < 8:
                     load_mask((i + 3) // 4 + 2)
+            if i + 3 < NCH:
+                turn = turns.tile([P, NR], F32, tag="turn", name="turn%d" % (i + 3))
+                nc.vector.tensor_copy(out=turn[:], in_=negr[:])
+                pool_squares(i + 3, turn)
             if 1 <= i <= NCH:
                 matmul_one(i - 1)
             if 2 <= i <= NCH + 1:
                 matmul_two(i - 2)
             if i >= 3:
-                o_out(i - 3, "vs" if i >= NCH else "vv")
+                o_out(i - 3, "vs" if i % 2 == 1 or i >= NCH else "vv")

@@ -22,7 +22,9 @@ G, J = 16, 8
 CH = 128
 CPN = B // CH
 NCH = NCLOUD * CPN
+NPAIR = NCH // 2
 COLS = CH * NT
+S_RADII = 5
 FLOPS = 2 * NCLOUD * C * A * B * NR + 2 * NCLOUD * D * C * NR * B
 
 
@@ -60,7 +62,7 @@ def tile_se3pointconvolution_t_kernel(tc, feat, diff, mask, w, radii, out):
         in_codes = keep.tile([P, 1024], U32, name="in_codes", align_bytes=64)
         in_scales = keep.tile([P, 1024], U8, name="in_scales", align_bytes=64)
 
-        dist = [dpool.tile([P, COLS], F32, name="dist%d" % i) for i in range(NCH)]
+        dist = [dpool.tile([P, 2 * COLS], F32, name="dist%d" % j) for j in range(NPAIR)]
         mraw = {}
         mperm = {}
 
@@ -79,6 +81,17 @@ def tile_se3pointconvolution_t_kernel(tc, feat, diff, mask, w, radii, out):
                 in_=mraw[h][:].rearrange("p b (g t j) -> p t (b g) j", t=NT, j=J),
             )
             mperm[h] = t
+
+        zp = ctx.enter_context(tc.tile_pool(name="z", bufs=4))
+        z = {}
+
+        def new_z(i):
+            z[i] = zp.tile([P, NR, COLS], F32, tag="z", name="z%d" % i)
+
+        def act_squares(i):
+            d = dist[i // 2][:, (i % 2) * COLS : (i % 2 + 1) * COLS]
+            for r in range(S_RADII):
+                nc.scalar.activation(out=z[i][:, r, :], in_=d, func=ACT.Square, bias=negr[:, r : r + 1], scale=1.0)
 
         with tc.tile_pool(name="dm", bufs=6) as dmp, tc.tile_pool(name="sq", bufs=4) as sqp, tc.psum_pool(
             name="pps", bufs=4
@@ -123,10 +136,22 @@ def tile_se3pointconvolution_t_kernel(tc, feat, diff, mask, w, radii, out):
 
             def root(i):
                 nc.scalar.activation(
-                    out=dist[i][:].rearrange("p (b t) -> p b t", t=NT),
+                    out=dist[i // 2][:, (i % 2) * COLS : (i % 2 + 1) * COLS].rearrange("p (b t) -> p b t", t=NT),
                     in_=st[i][:].rearrange("p t b -> p b t"),
                     func=ACT.Sqrt,
                 )
+
+            def load_small():
+                nc.sync.dma_start(
+                    out=itmp[:, 0:1024].rearrange("p (j a) -> p j a", j=2),
+                    in_=feat.rearrange("n c a -> (n c) a").rearrange("(j p) a -> p j a", p=P),
+                )
+                nc.sync.dma_start(
+                    out=wtmp[:, 0:4096].rearrange("p (e k) -> p e k", e=8),
+                    in_=w.rearrange("(e p) c r -> p e (c r)", p=P),
+                )
+                for h in range(2):
+                    load_mask(h)
 
             warm = pps.tile([P, 512], F32, tag="warm", name="warm", bufs=1)
             for i in range(5):
@@ -136,27 +161,27 @@ def tile_se3pointconvolution_t_kernel(tc, feat, diff, mask, w, radii, out):
             for i in range(NCH + 2):
                 if i + 5 < NCH:
                     load_dm(i + 5)
+                if i + 5 == NCH:
+                    load_small()
                 if i < NCH:
                     squares(i)
                 if 1 <= i <= NCH:
                     sum_transpose(i - 1)
+                if i == NCH:
+                    new_z(0)
+                    act_squares(0)
                 if i >= 2:
                     root(i - 2)
 
-            nc.sync.dma_start(
-                out=itmp[:, 0:1024].rearrange("p (j a) -> p j a", j=2),
-                in_=feat.rearrange("n c a -> (n c) a").rearrange("(j p) a -> p j a", p=P),
-            )
-            nc.sync.dma_start(
-                out=wtmp[:, 0:4096].rearrange("p (e k) -> p e k", e=8),
-                in_=w.rearrange("(e p) c r -> p e (c r)", p=P),
-            )
-            for h in range(2):
-                load_mask(h)
             nc.vector.tensor_copy(
                 out=itmp[:, 1024:2048].rearrange("p (t n j) -> p t n j", t=NT, j=J),
                 in_=itmp[:, 0:1024].rearrange("p (n t j) -> p t n j", t=NT, j=J),
             )
+            for h in range(2):
+                permute_mask(h)
+                load_mask(h + 2)
+            first_turn = const.tile([P, NR], F32, name="first_turn")
+            nc.vector.tensor_copy(out=first_turn[:], in_=negr[:])
 
             inq = itmp[:, 4096:8192].rearrange("p (n h c two t) -> p n h c two t", n=NCLOUD, h=2, c=C, two=2)
             for j in range(2):
@@ -186,21 +211,15 @@ def tile_se3pointconvolution_t_kernel(tc, feat, diff, mask, w, radii, out):
                         out=in_codes[:].bitcast(FP8X4), scales=in_scales[:], in_=itmp[:, 4096:8192]
                     )
             nc.vector.quantize_mx(out=w_codes[:].bitcast(FP8X4), scales=w_scales[:], in_=wtmp[:, 4096:8192])
-            for h in range(2):
-                permute_mask(h)
-                load_mask(h + 2)
 
-        zp = ctx.enter_context(tc.tile_pool(name="z", bufs=4))
-        yp = ctx.enter_context(tc.tile_pool(name="y", bufs=2))
+        yp = ctx.enter_context(tc.tile_pool(name="y", bufs=1))
         rp = ctx.enter_context(tc.tile_pool(name="r", bufs=2))
         tp = ctx.enter_context(tc.tile_pool(name="t", bufs=2))
+        turns = ctx.enter_context(tc.tile_pool(name="turns", bufs=2))
         ps_m = ctx.enter_context(tc.psum_pool(name="ps_m", bufs=2))
         ps_t = ctx.enter_context(tc.psum_pool(name="ps_t", bufs=2))
-        ps_o = ctx.enter_context(tc.psum_pool(name="ps_o", bufs=2))
+        ps_o = ctx.enter_context(tc.psum_pool(name="ps_o", bufs=1))
 
-        turns = ctx.enter_context(tc.tile_pool(name="turns", bufs=2))
-
-        z = {}
         mt = {}
         rb = {}
         rc = {}
@@ -209,36 +228,28 @@ def tile_se3pointconvolution_t_kernel(tc, feat, diff, mask, w, radii, out):
         tcd = {}
         ops = {}
         sto = {}
+        G_RADII = NR - S_RADII
 
-        def first_pool_radius(i):
-            return 5
-
-        def pool_squares(i, turn):
-            first = first_pool_radius(i)
-            zt = zp.tile([P, NR, COLS], F32, tag="z", name="z%d" % i)
-            y = yp.tile([P, NR - first, COLS], F32, tag="y", name="y%d" % i)
-            for r in range(first, NR):
+        def pool_squares(j, turn):
+            y = yp.tile([P, G_RADII, 2 * COLS], F32, tag="y", name="y%d" % j)
+            for g in range(G_RADII):
+                r = S_RADII + g
                 nc.gpsimd.tensor_scalar(
-                    out=y[:, r - first, :],
-                    in0=dist[i][:],
-                    scalar1=turn[:, r : r + 1],
-                    scalar2=1.0,
-                    op0=ALU.add,
-                    op1=ALU.mult,
+                    out=y[:, g, :], in0=dist[j][:], scalar1=turn[:, r : r + 1], scalar2=1.0, op0=ALU.add, op1=ALU.mult
                 )
-            nc.gpsimd.tensor_tensor(out=zt[:, first:NR, :], in0=y[:], in1=y[:], op=ALU.mult)
-            z[i] = zt
+            for s in range(2):
+                i = 2 * j + s
+                if i > 0:
+                    new_z(i)
+                half = y[:, :, s * COLS : (s + 1) * COLS]
+                nc.gpsimd.tensor_tensor(out=z[i][:, S_RADII:NR, :], in0=half, in1=half, op=ALU.mult)
 
-        def act_squares(i):
-            for r in range(first_pool_radius(i)):
-                nc.scalar.activation(
-                    out=z[i][:, r, :], in_=dist[i][:], func=ACT.Square, bias=negr[:, r : r + 1], scale=1.0
-                )
-
-        def act_exp(i, h):
-            nc.scalar.activation(
-                out=z[i][:, 4 * h : 4 * h + 4, :], in_=z[i][:, 4 * h : 4 * h + 4, :], func=ACT.Exp, scale=-GAMMA
-            )
+        def exponentials(i):
+            if i > 0:
+                act_squares(i)
+            for h in range(2):
+                part = z[i][:, 4 * h : 4 * h + 4, :]
+                nc.scalar.activation(out=part, in_=part, func=ACT.Exp, scale=-GAMMA)
 
         def mask_transpose(i):
             m = ps_m.tile([P, NT, CH], BF16, tag="mt", name="mt%d" % i)
@@ -282,25 +293,26 @@ def tile_se3pointconvolution_t_kernel(tc, feat, diff, mask, w, radii, out):
             tps[i] = acc
 
         def t_out(i):
-            t = tp.tile([P, 512], BF16, tag="tb", name="tb%d" % i, align_bytes=64)
+            if i % 2 == 0:
+                tb[i // 2] = tp.tile([P, 1024], BF16, tag="tb", name="tb%d" % (i // 2), align_bytes=64)
             nc.vector.tensor_copy(
-                out=t[:].rearrange("p (b r) -> p b r", r=4), in_=tps[i][:].rearrange("p (r b) -> p b r", r=4)
+                out=tb[i // 2][:, (i % 2) * 512 : (i % 2 + 1) * 512].rearrange("p (b r) -> p b r", r=4),
+                in_=tps[i][:].rearrange("p (r b) -> p b r", r=4),
             )
-            tb[i] = t
 
-        def quant_t(i):
-            codes = tp.tile([P, CH], U32, tag="tc", name="tc%d" % i, align_bytes=64)
-            scales = tp.tile([P, CH], U8, tag="ts", name="ts%d" % i, align_bytes=64)
-            nc.vector.quantize_mx(out=codes[:].bitcast(FP8X4), scales=scales[:], in_=tb[i][:])
-            tcd[i] = (codes, scales)
+        def quant_t(j):
+            codes = tp.tile([P, 2 * CH], U32, tag="tc", name="tc%d" % j, align_bytes=64)
+            scales = tp.tile([P, 2 * CH], U8, tag="ts", name="ts%d" % j, align_bytes=64)
+            nc.vector.quantize_mx(out=codes[:].bitcast(FP8X4), scales=scales[:], in_=tb[j][:])
+            tcd[j] = (codes, scales)
 
-        def matmul_two(i):
-            codes, scales = tcd[i]
-            banks = []
-            for k in range(2):
-                o = ps_o.tile([P, 4, CH], F32, tag="o%d" % k, name="o%d_%d" % (k, i))
-                for e in range(4):
-                    lo = (4 * k + e) * P
+        def matmul_two(j):
+            codes, scales = tcd[j]
+            ops[j] = []
+            for q in range(4):
+                o = ps_o.tile([P, 2, 2 * CH], F32, tag="o%d" % q, name="o%d_%d" % (q, j))
+                for e in range(2):
+                    lo = (2 * q + e) * P
                     nc.tensor.matmul_mx(
                         out=o[:, e, :],
                         lhsT=w_codes[:, lo : lo + P].bitcast(FP8X4),
@@ -310,57 +322,85 @@ def tile_se3pointconvolution_t_kernel(tc, feat, diff, mask, w, radii, out):
                         start=True,
                         stop=True,
                     )
-                banks.append(o)
-            ops[i] = banks
+                ops[j].append(o)
 
-        def o_out(i, engines):
-            hf = i // 4
-            if i % 4 == 0:
+        def o_out(j, q, engine):
+            hf = j // 2
+            if j % 2 == 0 and q == 0:
                 sto[hf] = stage.tile([P, 8, 512], F32, tag="stage", name="sto%d" % hf, align_bytes=64)
-            cols = slice((i % 4) * CH, (i % 4 + 1) * CH)
-            for k in range(2):
-                if engines[k] == "v":
-                    nc.vector.tensor_copy(out=sto[hf][:, 4 * k : 4 * k + 4, cols], in_=ops[i][k][:])
-                else:
-                    nc.scalar.copy(out=sto[hf][:, 4 * k : 4 * k + 4, cols], in_=ops[i][k][:])
+            cols = slice((j % 2) * 256, (j % 2 + 1) * 256)
+            if engine == "v":
+                nc.vector.tensor_copy(out=sto[hf][:, 2 * q : 2 * q + 2, cols], in_=ops[j][q][:])
+            else:
+                nc.scalar.copy(out=sto[hf][:, 2 * q : 2 * q + 2, cols], in_=ops[j][q][:])
             dst = out[hf // 2].rearrange("(e p) b -> p e b", p=P)
             base = (hf % 2) * 512
             if hf == 7:
-                nc.sync.dma_start(out=dst[:, :, base + (i % 4) * CH : base + (i % 4 + 1) * CH], in_=sto[hf][:, :, cols])
-            elif i % 4 == 3:
+                if q % 2 == 1:
+                    lo = base + (j % 2) * 256
+                    nc.sync.dma_start(
+                        out=dst[:, 2 * q - 2 : 2 * q + 2, lo : lo + 256], in_=sto[hf][:, 2 * q - 2 : 2 * q + 2, cols]
+                    )
+            elif j % 2 == 1 and q == 3:
                 nc.sync.dma_start(out=dst[:, :, base : base + 512], in_=sto[hf][:])
 
-        for i in range(3):
-            pool_squares(i, negr)
-        mask_transpose(0)
-        for i in range(NCH + 3):
-            if i < NCH:
-                act_squares(i)
-                act_exp(i, 0)
-                act_exp(i, 1)
-            if i + 1 < NCH:
-                mask_transpose(i + 1)
-            if i < NCH:
-                weigh(i, 0)
-            if 2 <= i <= NCH + 1:
-                t_out(i - 2)
-            if i < NCH:
-                weigh(i, 1)
-            if 1 <= i <= NCH:
-                quant_r(i - 1)
-            if 2 <= i <= NCH + 1:
-                quant_t(i - 2)
-            if i % 4 == 1 and 2 <= (i + 3) // 4 < 8:
-                permute_mask((i + 3) // 4)
-                if (i + 3) // 4 + 2 < 8:
-                    load_mask((i + 3) // 4 + 2)
-            if i + 3 < NCH:
-                turn = turns.tile([P, NR], F32, tag="turn", name="turn%d" % (i + 3))
+        for j in range(2):
+            pool_squares(j, first_turn)
+        for i in range(2):
+            mask_transpose(i)
+        for j in range(NPAIR):
+            a, b = 2 * j, 2 * j + 1
+            final = j == NPAIR - 1
+            exponentials(a)
+            exponentials(b)
+            weigh(a, 0)
+            if j >= 1:
+                t_out(a - 2)
+            weigh(a, 1)
+            if not final:
+                mask_transpose(a + 2)
+            if j >= 2:
+                o_out(j - 2, 0, "v")
+                o_out(j - 2, 1, "v")
+            weigh(b, 0)
+            if j >= 1:
+                t_out(b - 2)
+            if j >= 2:
+                o_out(j - 2, 2, "v")
+                o_out(j - 2, 3, "s")
+            if final:
+                quant_r(a)
+                quant_t(j - 1)
+                matmul_one(a)
+                matmul_two(j - 1)
+            weigh(b, 1)
+            if not final:
+                mask_transpose(b + 2)
+                quant_r(a)
+                quant_r(b)
+                if j >= 1:
+                    quant_t(j - 1)
+            if j % 2 == 0 and 2 <= j // 2 + 1 < 8:
+                permute_mask(j // 2 + 1)
+                if j // 2 + 3 < 8:
+                    load_mask(j // 2 + 3)
+            if j + 2 < NPAIR:
+                turn = turns.tile([P, NR], F32, tag="turn", name="turn%d" % (j + 2))
                 nc.vector.tensor_copy(out=turn[:], in_=negr[:])
-                pool_squares(i + 3, turn)
-            if 1 <= i <= NCH:
-                matmul_one(i - 1)
-            if 2 <= i <= NCH + 1:
-                matmul_two(i - 2)
-            if i >= 3:
-                o_out(i - 3, "vs" if i % 2 == 1 or i >= NCH else "vv")
+                pool_squares(j + 2, turn)
+            if not final:
+                matmul_one(a)
+                matmul_one(b)
+                if j >= 1:
+                    matmul_two(j - 1)
+
+        t_out(NCH - 2)
+        quant_r(NCH - 1)
+        matmul_one(NCH - 1)
+        for q in range(4):
+            o_out(NPAIR - 2, q, "vsvs"[q])
+        t_out(NCH - 1)
+        quant_t(NPAIR - 1)
+        matmul_two(NPAIR - 1)
+        for q in range(4):
+            o_out(NPAIR - 1, q, "vsvs"[q])

@@ -367,7 +367,7 @@ def tile_se3pointconvolution_t_kernel(tc, feat, diff, mask, w, radii, out):
                 t_out(b - 2)
             if j >= 2:
                 o_out(j - 2, 2, "v")
-                o_out(j - 2, 3, "s")
+                o_out(j - 2, 3, "s" if j % 2 else "v")
             if final:
                 quant_r(a)
                 quant_t(j - 1)

from contextlib import ExitStack

import concourse.bass as bass
import concourse.mybir as mybir
import concourse.tile as tile
from concourse.masks import make_identity

F32 = mybir.dt.float32
BF16 = mybir.dt.bfloat16
U32 = mybir.dt.uint32
U8 = mybir.dt.uint8
I32 = mybir.dt.int32
FP8X4 = mybir.dt.float8_e4m3fn_x4
ACT = mybir.ActivationFunctionType
ALU = mybir.AluOpType

NCLOUD, B, A, C, D, NR, XD = 4, 1024, 512, 64, 1024, 8, 3
GAMMA = 6.125
P = 128
NT = A // P
G, J = 16, 8
CH = 128
CPN = B // CH
NCH = NCLOUD * CPN
NPAIR = NCH // 2
COLS = CH * NT
S_RADII = 5
FLOPS = 2 * NCLOUD * C * A * B * NR + 2 * NCLOUD * D * C * NR * B


def tile_se3pointconvolution_t_kernel(tc, feat, diff, mask, w, radii, out):
    nc = tc.nc
    with ExitStack() as ctx:
        ctx.enter_context(tc.manual_schedule())
        const = ctx.enter_context(tc.tile_pool(name="const", bufs=1))
        dpool = ctx.enter_context(tc.tile_pool(name="dist", bufs=1))
        keep = ctx.enter_context(tc.tile_pool(name="keep", bufs=1))
        stage = ctx.enter_context(tc.tile_pool(name="stage", bufs=2))
        mraw_pool = ctx.enter_context(tc.tile_pool(name="mraw", bufs=2))

        one = const.tile([P, 1], F32, name="one")
        junk = const.tile([P, 1], F32, name="junk")
        rad_b = const.tile([P, NR], BF16, name="rad_b")
        negr = const.tile([P, NR], F32, name="negr")
        ident_f = const.tile([P, P], F32, name="ident_f")
        ident_b = const.tile([P, P], BF16, name="ident_b")
        nc.scalar.dma_start(out=rad_b[:], in_=radii.partition_broadcast(P))
        zeros = const.tile([P, 512], BF16, name="zeros")
        nc.vector.memset(one[:], 1.0)
        nc.vector.memset(zeros[:], 0.0)
        nc.scalar.activation(out=junk[:], in_=one[:], func=ACT.Sqrt)
        make_identity(nc, ident_f[:])
        make_identity(nc, ident_b[:])

        wtmp = stage.tile([P, 8192], BF16, tag="stage", name="wtmp", align_bytes=64)
        itmp = stage.tile([P, 8192], BF16, tag="stage", name="itmp", align_bytes=64)
        nc.vector.memset(itmp[:, 4096:8192].bitcast(I32), 0)
        nc.vector.tensor_scalar(out=negr[:], in0=rad_b[:], scalar1=-1.0, scalar2=None, op0=ALU.mult)

        w_codes = keep.tile([P, D], U32, name="w_codes", align_bytes=64)
        w_scales = keep.tile([P, D], U8, name="w_scales", align_bytes=64)
        in_codes = keep.tile([P, 1024], U32, name="in_codes", align_bytes=64)
        in_scales = keep.tile([P, 1024], U8, name="in_scales", align_bytes=64)

        dist = [dpool.tile([P, 2 * COLS], F32, name="dist%d" % j) for j in range(NPAIR)]
        mraw = {}
        mperm = {}

        def load_mask(h):
            t = mraw_pool.tile([P, 4, A], BF16, tag="mraw", name="mraw%d" % h)
            nc.sync.dma_start(
                out=t[:],
                in_=mask[h // 2, (h % 2) * 512 : (h % 2 + 1) * 512, :].rearrange("(j p) a -> p j a", p=P),
            )
            mraw[h] = t

        def permute_mask(h):
            t = mraw_pool.tile([P, NT, 4 * P], BF16, tag="mperm", name="mperm%d" % h)
            nc.vector.tensor_copy(
                out=t[:].rearrange("p t (n j) -> p t n j", j=J),
                in_=mraw[h][:].rearrange("p b (g t j) -> p t (b g) j", t=NT, j=J),
            )
            mperm[h] = t

        zp = ctx.enter_context(tc.tile_pool(name="z", bufs=4))
        z = {}

        def new_z(i):
            z[i] = zp.tile([P, NR, COLS], F32, tag="z", name="z%d" % i)

        def act_squares(i):
            d = dist[i // 2][:, (i % 2) * COLS : (i % 2 + 1) * COLS]
            for r in range(S_RADII):
                nc.scalar.activation(out=z[i][:, r, :], in_=d, func=ACT.Square, bias=negr[:, r : r + 1], scale=1.0)

        with tc.tile_pool(name="dm", bufs=6) as dmp, tc.tile_pool(name="sq", bufs=4) as sqp, tc.psum_pool(
            name="pps", bufs=4
        ) as pps:
            dm = {}
            sq = {}
            st = {}

            def load_dm(i):
                t = dmp.tile([P, A * XD], BF16, tag="dm", name="dm%d" % i)
                nc.sync.dma_start(
                    out=t[:], in_=diff[i // CPN, (i % CPN) * CH : (i % CPN + 1) * CH].rearrange("b a x -> b (a x)")
                )
                dm[i] = t

            def squares(i):
                v = dm[i][:].rearrange("p (g t j x) -> p x t g j", g=G, t=NT, j=J)
                s = sqp.tile([P, XD, A], F32, tag="sq", name="sq%d" % i)
                so = [s[:, x, :].rearrange("p (t g j) -> p t g j", t=NT, g=G) for x in range(XD)]
                for x in range(2):
                    nc.vector.tensor_tensor(out=so[x], in0=v[:, x], in1=v[:, x], op=ALU.mult)
                nc.scalar.activation(out=so[2], in_=v[:, 2], func=ACT.Square)
                sq[i] = s

            def keep_clock(n):
                nc.tensor.matmul(out=warm[:, 0:n], lhsT=ident_b[:], rhs=zeros[:, 0:n], start=True, stop=True)

            def sum_transpose(i):
                t_ps = pps.tile([P, NT, CH], F32, tag="st", name="st%d" % i)
                for t in range(NT):
                    for x in range(XD):
                        nc.tensor.matmul(
                            out=t_ps[:, t, :],
                            lhsT=sq[i][:, x, t * P : (t + 1) * P],
                            rhs=ident_f[:],
                            is_transpose=True,
                            start=(x == 0),
                            stop=(x == XD - 1),
                        )
                keep_clock(512)
                st[i] = t_ps

            def root(i):
                nc.scalar.activation(
                    out=dist[i // 2][:, (i % 2) * COLS : (i % 2 + 1) * COLS].rearrange("p (b t) -> p b t", t=NT),
                    in_=st[i][:].rearrange("p t b -> p b t"),
                    func=ACT.Sqrt,
                )

            def load_small():
                nc.sync.dma_start(
                    out=itmp[:, 0:1024].rearrange("p (j a) -> p j a", j=2),
                    in_=feat.rearrange("n c a -> (n c) a").rearrange("(j p) a -> p j a", p=P),
                )
                nc.sync.dma_start(
                    out=wtmp[:, 0:4096].rearrange("p (e k) -> p e k", e=8),
                    in_=w.rearrange("(e p) c r -> p e (c r)", p=P),
                )
                for h in range(2):
                    load_mask(h)

            warm = pps.tile([P, 512], F32, tag="warm", name="warm", bufs=1)
            for i in range(5):
                load_dm(i)
            for i in range(4):
                keep_clock(512)
            for i in range(NCH + 2):
                if i + 5 < NCH:
                    load_dm(i + 5)
                if i + 5 == NCH:
                    load_small()
                if i < NCH:
                    squares(i)
                if 1 <= i <= NCH:
                    sum_transpose(i - 1)
                if i == NCH:
                    new_z(0)
                    act_squares(0)
                if i >= 2:
                    root(i - 2)

            nc.vector.tensor_copy(
                out=itmp[:, 1024:2048].rearrange("p (t n j) -> p t n j", t=NT, j=J),
                in_=itmp[:, 0:1024].rearrange("p (n t j) -> p t n j", t=NT, j=J),
            )
            for h in range(2):
                permute_mask(h)
                load_mask(h + 2)
            first_turn = const.tile([P, NR], F32, name="first_turn")
            nc.vector.tensor_copy(out=first_turn[:], in_=negr[:])

            inq = itmp[:, 4096:8192].rearrange("p (n h c two t) -> p n h c two t", n=NCLOUD, h=2, c=C, two=2)
            for j in range(2):
                ips = pps.tile([P, NT, P], BF16, tag="prep", name="ips%d" % j, bufs=3)
                for t in range(NT):
                    nc.tensor.transpose(
                        out=ips[:, t, :], in_=itmp[:, 1024 + t * 256 + j * P : 1024 + t * 256 + (j + 1) * P], identity=ident_b[:]
                    )
                for n2 in range(2):
                    for h in range(2):
                        nc.vector.tensor_copy(
                            out=inq[:, 2 * j + n2, h, :, h, :],
                            in_=ips[:, :, n2 * C : (n2 + 1) * C].rearrange("p t c -> p c t"),
                        )
            w_words = wtmp[:, 0:4096].bitcast(F32).rearrange("p (e q u) -> p e u q", e=8, u=2)
            w_grouped = wtmp[:, 4096:8192].bitcast(F32).rearrange("p (e d u) -> p e d u", e=8, u=2)
            for k in range(4):
                wps = pps.tile([P, 2, 2, P], F32, tag="prep", name="wps%d" % k, bufs=3)
                for e in range(2):
                    for u in range(2):
                        nc.tensor.transpose(out=wps[:, e, u, :], in_=w_words[:, 2 * k + e, u, :], identity=ident_f[:])
                nc.vector.tensor_copy(
                    out=w_grouped[:, 2 * k : 2 * k + 2, :, :], in_=wps[:].rearrange("p e u d -> p e d u")
                )
                if k == 0:
                    nc.vector.quantize_mx(
                        out=in_codes[:].bitcast(FP8X4), scales=in_scales[:], in_=itmp[:, 4096:8192]
                    )
            nc.vector.quantize_mx(out=w_codes[:].bitcast(FP8X4), scales=w_scales[:], in_=wtmp[:, 4096:8192])

        yp = ctx.enter_context(tc.tile_pool(name="y", bufs=1))
        rp = ctx.enter_context(tc.tile_pool(name="r", bufs=2))
        tp = ctx.enter_context(tc.tile_pool(name="t", bufs=2))
        turns = ctx.enter_context(tc.tile_pool(name="turns", bufs=2))
        ps_m = ctx.enter_context(tc.psum_pool(name="ps_m", bufs=2))
        ps_t = ctx.enter_context(tc.psum_pool(name="ps_t", bufs=2))
        ps_o = ctx.enter_context(tc.psum_pool(name="ps_o", bufs=1))

        mt = {}
        rb = {}
        rc = {}
        tps = {}
        tb = {}
        tcd = {}
        ops = {}
        sto = {}
        G_RADII = NR - S_RADII

        def pool_squares(j, turn):
            y = yp.tile([P, G_RADII, 2 * COLS], F32, tag="y", name="y%d" % j)
            for g in range(G_RADII):
                r = S_RADII + g
                nc.gpsimd.tensor_scalar(
                    out=y[:, g, :], in0=dist[j][:], scalar1=turn[:, r : r + 1], scalar2=1.0, op0=ALU.add, op1=ALU.mult
                )
            for s in range(2):
                i = 2 * j + s
                if i > 0:
                    new_z(i)
                half = y[:, :, s * COLS : (s + 1) * COLS]
                nc.gpsimd.tensor_tensor(out=z[i][:, S_RADII:NR, :], in0=half, in1=half, op=ALU.mult)

        def exponentials(i):
            if i > 0:
                act_squares(i)
            for h in range(2):
                part = z[i][:, 4 * h : 4 * h + 4, :]
                nc.scalar.activation(out=part, in_=part, func=ACT.Exp, scale=-GAMMA)

        def mask_transpose(i):
            m = ps_m.tile([P, NT, CH], BF16, tag="mt", name="mt%d" % i)
            for t in range(NT):
                nc.tensor.transpose(
                    out=m[:, t, :], in_=mperm[i // 4][:, t, (i % 4) * P : (i % 4 + 1) * P], identity=ident_b[:]
                )
            mt[i] = m

        def weigh(i, h):
            if h == 0:
                rb[i] = rp.tile([P, NR * COLS], BF16, tag="rb", name="rb%d" % i, align_bytes=64)
            nc.vector.tensor_tensor(
                out=rb[i][:, h * 2048 : (h + 1) * 2048].rearrange("p (r b t) -> p r b t", r=4, t=NT),
                in0=z[i][:, 4 * h : 4 * h + 4, :].rearrange("p r (b t) -> p r b t", t=NT),
                in1=mt[i][:].rearrange("p t b -> p b t").unsqueeze(1).to_broadcast([P, 4, CH, NT]),
                op=ALU.mult,
            )

        def quant_r(i):
            codes = rp.tile([P, 1024], U32, tag="rc", name="rc%d" % i, align_bytes=64)
            scales = rp.tile([P, 1024], U8, tag="rs", name="rs%d" % i, align_bytes=64)
            nc.vector.quantize_mx(out=codes[:].bitcast(FP8X4), scales=scales[:], in_=rb[i][:])
            rc[i] = (codes, scales)

        def matmul_one(i):
            n = i // CPN
            acc = ps_t.tile([P, 512], F32, tag="tps", name="tps%d" % i)
            codes, scales = rc[i]
            for h in range(2):
                lo = (2 * n + h) * P
                nc.tensor.matmul_mx(
                    out=acc[:],
                    lhsT=in_codes[:, lo : lo + P].bitcast(FP8X4),
                    lhsT_scale=in_scales[:, lo : lo + P],
                    rhs=codes[:, h * 512 : (h + 1) * 512].bitcast(FP8X4),
                    rhs_scale=scales[:, h * 512 : (h + 1) * 512],
                    start=(h == 0),
                    stop=(h == 1),
                )
            tps[i] = acc

        def t_out(i):
            if i % 2 == 0:
                tb[i // 2] = tp.tile([P, 1024], BF16, tag="tb", name="tb%d" % (i // 2), align_bytes=64)
            nc.vector.tensor_copy(
                out=tb[i // 2][:, (i % 2) * 512 : (i % 2 + 1) * 512].rearrange("p (b r) -> p b r", r=4),
                in_=tps[i][:].rearrange("p (r b) -> p b r", r=4),
            )

        def quant_t(j):
            codes = tp.tile([P, 2 * CH], U32, tag="tc", name="tc%d" % j, align_bytes=64)
            scales = tp.tile([P, 2 * CH], U8, tag="ts", name="ts%d" % j, align_bytes=64)
            nc.vector.quantize_mx(out=codes[:].bitcast(FP8X4), scales=scales[:], in_=tb[j][:])
            tcd[j] = (codes, scales)

        def matmul_two(j):
            codes, scales = tcd[j]
            ops[j] = []
            for q in range(4):
                o = ps_o.tile([P, 2, 2 * CH], F32, tag="o%d" % q, name="o%d_%d" % (q, j))
                for e in range(2):
                    lo = (2 * q + e) * P
                    nc.tensor.matmul_mx(
                        out=o[:, e, :],
                        lhsT=w_codes[:, lo : lo + P].bitcast(FP8X4),
                        lhsT_scale=w_scales[:, lo : lo + P],
                        rhs=codes[:].bitcast(FP8X4),
                        rhs_scale=scales[:],
                        start=True,
                        stop=True,
                    )
                ops[j].append(o)

        def o_out(j, q, engine):
            hf = j // 2
            if j % 2 == 0 and q == 0:
                sto[hf] = stage.tile([P, 8, 512], F32, tag="stage", name="sto%d" % hf, align_bytes=64)
            cols = slice((j % 2) * 256, (j % 2 + 1) * 256)
            if engine == "v":
                nc.vector.tensor_copy(out=sto[hf][:, 2 * q : 2 * q + 2, cols], in_=ops[j][q][:])
            else:
                nc.scalar.copy(out=sto[hf][:, 2 * q : 2 * q + 2, cols], in_=ops[j][q][:])
            dst = out[hf // 2].rearrange("(e p) b -> p e b", p=P)
            base = (hf % 2) * 512
            if hf == 7:
                if q % 2 == 1:
                    lo = base + (j % 2) * 256
                    nc.sync.dma_start(
                        out=dst[:, 2 * q - 2 : 2 * q + 2, lo : lo + 256], in_=sto[hf][:, 2 * q - 2 : 2 * q + 2, cols]
                    )
            elif j % 2 == 1 and q == 3:
                nc.sync.dma_start(out=dst[:, :, base : base + 512], in_=sto[hf][:])

        for j in range(2):
            pool_squares(j, first_turn)
        for i in range(2):
            mask_transpose(i)
        for j in range(NPAIR):
            a, b = 2 * j, 2 * j + 1
            final = j == NPAIR - 1
            exponentials(a)
            exponentials(b)
            weigh(a, 0)
            if j >= 1:
                t_out(a - 2)
            weigh(a, 1)
            if not final:
                mask_transpose(a + 2)
            if j >= 2:
                o_out(j - 2, 0, "v")
                o_out(j - 2, 1, "v")
            weigh(b, 0)
            if j >= 1:
                t_out(b - 2)
            if j >= 2:
                o_out(j - 2, 2, "v")
                o_out(j - 2, 3, "s" if j % 2 else "v")
            if final:
                quant_r(a)
                quant_t(j - 1)
                matmul_one(a)
                matmul_two(j - 1)
            weigh(b, 1)
            if not final:
                mask_transpose(b + 2)
                quant_r(a)
                quant_r(b)
                if j >= 1:
                    quant_t(j - 1)
            if j % 2 == 0 and 2 <= j // 2 + 1 < 8:
                permute_mask(j // 2 + 1)
                if j // 2 + 3 < 8:
                    load_mask(j // 2 + 3)
            if j + 2 < NPAIR:
                turn = turns.tile([P, NR], F32, tag="turn", name="turn%d" % (j + 2))
                nc.vector.tensor_copy(out=turn[:], in_=negr[:])
                pool_squares(j + 2, turn)
            if not final:
                matmul_one(a)
                matmul_one(b)
                if j >= 1:
                    matmul_two(j - 1)

        t_out(NCH - 2)
        quant_r(NCH - 1)
        matmul_one(NCH - 1)
        for q in range(4):
            o_out(NPAIR - 2, q, "vsvs"[q])
        t_out(NCH - 1)
        quant_t(NPAIR - 1)
        matmul_two(NPAIR - 1)
        for q in range(4):
            o_out(NPAIR - 1, q, "vsvs"[q])
